import numpy as np
import ml_dtypes

BF16 = ml_dtypes.bfloat16


def bf(x):
    return np.asarray(x, np.float32).astype(BF16)


def f32(x):
    return np.asarray(x, np.float32)


def f64(x):
    return np.asarray(x).astype(np.float64)


def striped(idx):
    return np.tile(idx.reshape(-1, 16).T, (8, 1))


C, H, H2, S, N = 128, 128, 256, 512, 1024


def setup_inputs():
    return {
        "z": bf(np.random.standard_normal((C, S))),
        "w_in": bf(np.random.standard_normal((C, H)) / np.sqrt(C)),
        "b_in": f32(0.3 * np.random.standard_normal((H, 1))),
        "pool": bf(np.random.standard_normal((H, H2)) * np.sqrt(2.0 / H)),
        "cb": f32(0.3 * np.random.standard_normal((H2, 1))),
        "e1": f32(np.random.standard_normal((1, N))),
        "e2": f32(np.random.standard_normal((1, N))),
        "w_out": bf(1.5 * np.random.standard_normal((H, C)) / np.sqrt(H)),
        "b_out": f32(0.3 * np.random.standard_normal((C, 1))),
        "offs": striped(np.random.permutation(np.tile(np.arange(S), 2))[:N]),
    }


def reference(z, w_in, b_in, pool, cb, e1, e2, w_out, b_out, offs):
    idx = offs[:16].T.reshape(-1)
    h = np.maximum(f64(w_in).T @ f64(z)[:, idx] + f64(b_in), 0.0)
    u = f64(pool).T @ h + f64(cb)
    y = np.tanh(f64(e1) * u[:H] - f64(e2) * u[H:])
    return np.tanh(f64(w_out).T @ y + f64(b_out))

@@ -1,0 +1,76 @@
+import concourse.mybir as mybir
+
+BF16 = mybir.dt.bfloat16
+F32 = mybir.dt.float32
+U16 = mybir.dt.uint16
+RELU = mybir.ActivationFunctionType.Relu
+TANH = mybir.ActivationFunctionType.Tanh
+ADD = mybir.AluOpType.add
+MULT = mybir.AluOpType.mult
+SUBTRACT = mybir.AluOpType.subtract
+
+P = 128
+S = 512
+N = 1024
+PIECE = 512
+FLOPS = 2 * N * (P * P + P * 2 * P + P * P)
+
+
+def tile_vectorfield_g_kernel(tc, z, w_in, b_in, pooled, cb, e1, e2, w_out, b_out, offs, out):
+    nc = tc.nc
+    with (
+        tc.tile_pool(name="held", bufs=1) as held,
+        tc.tile_pool(name="work", bufs=2) as work,
+        tc.psum_pool(name="psum", bufs=2) as psum,
+    ):
+        offsets = held.tile([P, N // 16], U16, name="offsets")
+        nc.sync.dma_start(offsets[:], offs)
+        z_sb = held.tile([P, S], BF16, name="z_sb")
+        nc.sync.dma_start(z_sb[:], z)
+        w_in_sb = held.tile([P, P], BF16, name="w_in_sb")
+        nc.scalar.dma_start(w_in_sb[:], w_in)
+        b_in_sb = held.tile([P, 1], F32, name="b_in_sb")
+        nc.scalar.dma_start(b_in_sb[:], b_in)
+        pooled_sb = held.tile([P, 2 * P], BF16, name="pooled_sb")
+        nc.scalar.dma_start(pooled_sb[:], pooled)
+        cb1_sb = held.tile([P, 1], F32, name="cb1_sb")
+        nc.scalar.dma_start(cb1_sb[:], cb[0:P, :])
+        cb2_sb = held.tile([P, 1], F32, name="cb2_sb")
+        nc.scalar.dma_start(cb2_sb[:], cb[P : 2 * P, :])
+        e1_all = held.tile([P, N], F32, name="e1_all")
+        nc.sync.dma_start(e1_all[:], e1.broadcast_to([P, N]))
+        e2_all = held.tile([P, N], F32, name="e2_all")
+        nc.gpsimd.dma_start(e2_all[:], e2.broadcast_to([P, N]))
+        w_out_sb = held.tile([P, P], BF16, name="w_out_sb")
+        nc.scalar.dma_start(w_out_sb[:], w_out)
+        b_out_sb = held.tile([P, 1], F32, name="b_out_sb")
+        nc.scalar.dma_start(b_out_sb[:], b_out)
+
+        for first in range(0, N, PIECE):
+            cols = slice(first, first + PIECE)
+
+            h_ps = psum.tile([P, PIECE], F32, name="h_ps")
+            picked = z_sb[:].indirect(offsets[:, first // 16 : (first + PIECE) // 16])
+            nc.tensor.matmul(h_ps[:], w_in_sb[:], picked, start=True, stop=True)
+            h_sb = work.tile([P, PIECE], BF16, name="h_sb")
+            nc.scalar.activation(h_sb[:], h_ps[:], RELU, bias=b_in_sb[:])
+
+            u1_ps = psum.tile([P, PIECE], F32, name="u1_ps")
+            nc.tensor.matmul(u1_ps[:], pooled_sb[:, 0:P], h_sb[:], start=True, stop=True)
+            u2_ps = psum.tile([P, PIECE], F32, name="u2_ps")
+            nc.tensor.matmul(u2_ps[:], pooled_sb[:, P : 2 * P], h_sb[:], start=True, stop=True)
+
+            t1 = work.tile([P, PIECE], F32, name="t1")
+            nc.vector.scalar_tensor_tensor(t1[:], u1_ps[:], cb1_sb[:], e1_all[:, cols], op0=ADD, op1=MULT)
+            t2 = work.tile([P, PIECE], F32, name="t2")
+            nc.vector.scalar_tensor_tensor(t2[:], u2_ps[:], cb2_sb[:], e2_all[:, cols], op0=ADD, op1=MULT)
+            mixed = work.tile([P, PIECE], F32, name="mixed")
+            nc.vector.tensor_tensor(mixed[:], t1[:], t2[:], SUBTRACT)
+            y_sb = work.tile([P, PIECE], BF16, name="y_sb")
+            nc.scalar.activation(y_sb[:], mixed[:], TANH)
+
+            o_ps = psum.tile([P, PIECE], F32, name="o_ps")
+            nc.tensor.matmul(o_ps[:], w_out_sb[:], y_sb[:], start=True, stop=True)
+            o_sb = work.tile([P, PIECE], F32, name="o_sb")
+            nc.scalar.activation(o_sb[:], o_ps[:], TANH, bias=b_out_sb[:])
+            nc.sync.dma_start(out[:, cols], o_sb[:])

@@ -23,6 +23,11 @@ def tile_vectorfield_g_kernel(tc, z, w_in, b_in, pooled, cb, e1, e2, w_out, b_ou
         tc.tile_pool(name="work", bufs=2) as work,
         tc.psum_pool(name="psum", bufs=2) as psum,
     ):
+        zero = held.tile([P, 1], F32, name="zero")
+        nc.vector.memset(zero[:], 0.0)
+        warm = held.tile([P, 1], F32, name="warm")
+        nc.scalar.activation(warm[:], zero[:], TANH)
+
         offsets = held.tile([P, N // 16], U16, name="offsets")
         nc.sync.dma_start(offsets[:], offs)
         z_sb = held.tile([P, S], BF16, name="z_sb")
@@ -40,7 +45,7 @@ def tile_vectorfield_g_kernel(tc, z, w_in, b_in, pooled, cb, e1, e2, w_out, b_ou
         e1_all = held.tile([P, N], F32, name="e1_all")
         nc.sync.dma_start(e1_all[:], e1.broadcast_to([P, N]))
         e2_all = held.tile([P, N], F32, name="e2_all")
-        nc.gpsimd.dma_start(e2_all[:], e2.broadcast_to([P, N]))
+        nc.scalar.dma_start(e2_all[:], e2.broadcast_to([P, N]))
         w_out_sb = held.tile([P, P], BF16, name="w_out_sb")
         nc.scalar.dma_start(w_out_sb[:], w_out)
         b_out_sb = held.tile([P, 1], F32, name="b_out_sb")

@@ -12,7 +12,9 @@ SUBTRACT = mybir.AluOpType.subtract
 P = 128
 S = 512
 N = 1024
-PIECE = 512
+PIECE = 256
+PIECES = N // PIECE
+HALF = N // 2
 FLOPS = 2 * N * (P * P + P * 2 * P + P * P)
 
 
@@ -20,14 +22,10 @@ def tile_vectorfield_g_kernel(tc, z, w_in, b_in, pooled, cb, e1, e2, w_out, b_ou
     nc = tc.nc
     with (
         tc.tile_pool(name="held", bufs=1) as held,
-        tc.tile_pool(name="work", bufs=2) as work,
+        tc.tile_pool(name="work", bufs=PIECES) as work,
+        tc.psum_pool(name="psum_h", bufs=PIECES) as psum_h,
         tc.psum_pool(name="psum", bufs=2) as psum,
     ):
-        zero = held.tile([P, 1], F32, name="zero")
-        nc.vector.memset(zero[:], 0.0)
-        warm = held.tile([P, 1], F32, name="warm")
-        nc.scalar.activation(warm[:], zero[:], TANH)
-
         offsets = held.tile([P, N // 16], U16, name="offsets")
         nc.sync.dma_start(offsets[:], offs)
         z_sb = held.tile([P, S], BF16, name="z_sb")
@@ -38,37 +36,49 @@ def tile_vectorfield_g_kernel(tc, z, w_in, b_in, pooled, cb, e1, e2, w_out, b_ou
         nc.scalar.dma_start(b_in_sb[:], b_in)
         pooled_sb = held.tile([P, 2 * P], BF16, name="pooled_sb")
         nc.scalar.dma_start(pooled_sb[:], pooled)
-        cb1_sb = held.tile([P, 1], F32, name="cb1_sb")
-        nc.scalar.dma_start(cb1_sb[:], cb[0:P, :])
-        cb2_sb = held.tile([P, 1], F32, name="cb2_sb")
-        nc.scalar.dma_start(cb2_sb[:], cb[P : 2 * P, :])
-        e1_all = held.tile([P, N], F32, name="e1_all")
-        nc.sync.dma_start(e1_all[:], e1.broadcast_to([P, N]))
-        e2_all = held.tile([P, N], F32, name="e2_all")
-        nc.scalar.dma_start(e2_all[:], e2.broadcast_to([P, N]))
+        cb_sb = held.tile([P, 2], F32, name="cb_sb")
+        with nc.allow_non_contiguous_dma(reason="two bias columns, one float32 to a partition each"):
+            nc.gpsimd.dma_start(cb_sb[:], cb.rearrange("(t p) o -> p (t o)", t=2))
         w_out_sb = held.tile([P, P], BF16, name="w_out_sb")
-        nc.scalar.dma_start(w_out_sb[:], w_out)
+        nc.gpsimd.dma_start(w_out_sb[:], w_out)
         b_out_sb = held.tile([P, 1], F32, name="b_out_sb")
-        nc.scalar.dma_start(b_out_sb[:], b_out)
+        nc.gpsimd.dma_start(b_out_sb[:], b_out)
+        e1_half = [held.tile([P, HALF], F32, name=f"e1_half{i}") for i in range(2)]
+        e2_half = [held.tile([P, HALF], F32, name=f"e2_half{i}") for i in range(2)]
+        for i in range(2):
+            cols = slice(i * HALF, (i + 1) * HALF)
+            nc.sync.dma_start(e1_half[i][:], e1[:, cols].broadcast_to([P, HALF]))
+            nc.sync.dma_start(e2_half[i][:], e2[:, cols].broadcast_to([P, HALF]))
 
-        for first in range(0, N, PIECE):
-            cols = slice(first, first + PIECE)
+        zeros = held.tile([P, 1], BF16, name="zeros")
+        nc.vector.memset(zeros[:], 0.0)
+        warm_sb = held.tile([P, 1], F32, name="warm_sb")
+        nc.scalar.activation(warm_sb[:], zeros[:, 0:1], TANH)
 
-            h_ps = psum.tile([P, PIECE], F32, name="h_ps")
-            picked = z_sb[:].indirect(offsets[:, first // 16 : (first + PIECE) // 16])
-            nc.tensor.matmul(h_ps[:], w_in_sb[:], picked, start=True, stop=True)
+        h_ps = [psum_h.tile([P, PIECE], F32, name="h_ps") for k in range(PIECES)]
+        for k in range(PIECES):
+            picked = z_sb[:].indirect(offsets[:, k * PIECE // 16 : (k + 1) * PIECE // 16])
+            nc.tensor.matmul(h_ps[k][:], w_in_sb[:], picked, start=True, stop=True)
+
+        for k in range(PIECES):
+            half, first = divmod(k * PIECE, HALF)
+            e_cols = slice(first, first + PIECE)
+
             h_sb = work.tile([P, PIECE], BF16, name="h_sb")
-            nc.scalar.activation(h_sb[:], h_ps[:], RELU, bias=b_in_sb[:])
+            nc.scalar.activation(h_sb[:], h_ps[k][:], RELU, bias=b_in_sb[:])
 
-            u1_ps = psum.tile([P, PIECE], F32, name="u1_ps")
-            nc.tensor.matmul(u1_ps[:], pooled_sb[:, 0:P], h_sb[:], start=True, stop=True)
-            u2_ps = psum.tile([P, PIECE], F32, name="u2_ps")
-            nc.tensor.matmul(u2_ps[:], pooled_sb[:, P : 2 * P], h_sb[:], start=True, stop=True)
+            u_ps = psum.tile([P, 2 * PIECE], F32, name="u_ps")
+            nc.tensor.matmul(u_ps[:, 0:PIECE], pooled_sb[:, 0:P], h_sb[:], start=True, stop=True)
+            nc.tensor.matmul(u_ps[:, PIECE : 2 * PIECE], pooled_sb[:, P : 2 * P], h_sb[:], start=True, stop=True)
 
             t1 = work.tile([P, PIECE], F32, name="t1")
-            nc.vector.scalar_tensor_tensor(t1[:], u1_ps[:], cb1_sb[:], e1_all[:, cols], op0=ADD, op1=MULT)
+            nc.vector.scalar_tensor_tensor(
+                t1[:], u_ps[:, 0:PIECE], cb_sb[:, 0:1], e1_half[half][:, e_cols], op0=ADD, op1=MULT
+            )
             t2 = work.tile([P, PIECE], F32, name="t2")
-            nc.vector.scalar_tensor_tensor(t2[:], u2_ps[:], cb2_sb[:], e2_all[:, cols], op0=ADD, op1=MULT)
+            nc.vector.scalar_tensor_tensor(
+                t2[:], u_ps[:, PIECE : 2 * PIECE], cb_sb[:, 1:2], e2_half[half][:, e_cols], op0=ADD, op1=MULT
+            )
             mixed = work.tile([P, PIECE], F32, name="mixed")
             nc.vector.tensor_tensor(mixed[:], t1[:], t2[:], SUBTRACT)
             y_sb = work.tile([P, PIECE], BF16, name="y_sb")
@@ -78,4 +88,4 @@ def tile_vectorfield_g_kernel(tc, z, w_in, b_in, pooled, cb, e1, e2, w_out, b_ou
             nc.tensor.matmul(o_ps[:], w_out_sb[:], y_sb[:], start=True, stop=True)
             o_sb = work.tile([P, PIECE], F32, name="o_sb")
             nc.scalar.activation(o_sb[:], o_ps[:], TANH, bias=b_out_sb[:])
-            nc.sync.dma_start(out[:, cols], o_sb[:])
+            nc.sync.dma_start(out[:, k * PIECE : (k + 1) * PIECE], o_sb[:])

@@ -15,6 +15,8 @@ N = 1024
 PIECE = 256
 PIECES = N // PIECE
 HALF = N // 2
+BANK = 512
+WARM_MATMULS = 4
 FLOPS = 2 * N * (P * P + P * 2 * P + P * P)
 
 
@@ -50,10 +52,14 @@ def tile_vectorfield_g_kernel(tc, z, w_in, b_in, pooled, cb, e1, e2, w_out, b_ou
             nc.sync.dma_start(e1_half[i][:], e1[:, cols].broadcast_to([P, HALF]))
             nc.sync.dma_start(e2_half[i][:], e2[:, cols].broadcast_to([P, HALF]))
 
-        zeros = held.tile([P, 1], BF16, name="zeros")
+        zeros = held.tile([P, BANK], BF16, name="zeros")
         nc.vector.memset(zeros[:], 0.0)
         warm_sb = held.tile([P, 1], F32, name="warm_sb")
         nc.scalar.activation(warm_sb[:], zeros[:, 0:1], TANH)
+
+        warm_ps = psum.tile([P, BANK], F32, name="warm_ps", tag="o_ps")
+        for i in range(WARM_MATMULS):
+            nc.tensor.matmul(warm_ps[:], zeros[:, 0:P], zeros[:], start=True, stop=True)
 
         h_ps = [psum_h.tile([P, PIECE], F32, name="h_ps") for k in range(PIECES)]
         for k in range(PIECES):

@@ -16,7 +16,7 @@ PIECE = 256
 PIECES = N // PIECE
 HALF = N // 2
 BANK = 512
-WARM_MATMULS = 4
+WARM_MATMULS = 3
 FLOPS = 2 * N * (P * P + P * 2 * P + P * P)
 
 
@@ -28,10 +28,10 @@ def tile_vectorfield_g_kernel(tc, z, w_in, b_in, pooled, cb, e1, e2, w_out, b_ou
         tc.psum_pool(name="psum_h", bufs=PIECES) as psum_h,
         tc.psum_pool(name="psum", bufs=2) as psum,
     ):
-        offsets = held.tile([P, N // 16], U16, name="offsets")
-        nc.sync.dma_start(offsets[:], offs)
         z_sb = held.tile([P, S], BF16, name="z_sb")
         nc.sync.dma_start(z_sb[:], z)
+        offsets = held.tile([P, N // 16], U16, name="offsets")
+        nc.sync.dma_start(offsets[:], offs)
         w_in_sb = held.tile([P, P], BF16, name="w_in_sb")
         nc.scalar.dma_start(w_in_sb[:], w_in)
         b_in_sb = held.tile([P, 1], F32, name="b_in_sb")
@@ -40,17 +40,17 @@ def tile_vectorfield_g_kernel(tc, z, w_in, b_in, pooled, cb, e1, e2, w_out, b_ou
         nc.scalar.dma_start(pooled_sb[:], pooled)
         cb_sb = held.tile([P, 2], F32, name="cb_sb")
         with nc.allow_non_contiguous_dma(reason="two bias columns, one float32 to a partition each"):
-            nc.gpsimd.dma_start(cb_sb[:], cb.rearrange("(t p) o -> p (t o)", t=2))
-        w_out_sb = held.tile([P, P], BF16, name="w_out_sb")
-        nc.gpsimd.dma_start(w_out_sb[:], w_out)
-        b_out_sb = held.tile([P, 1], F32, name="b_out_sb")
-        nc.gpsimd.dma_start(b_out_sb[:], b_out)
+            nc.scalar.dma_start(cb_sb[:], cb.rearrange("(t p) o -> p (t o)", t=2))
         e1_half = [held.tile([P, HALF], F32, name=f"e1_half{i}") for i in range(2)]
         e2_half = [held.tile([P, HALF], F32, name=f"e2_half{i}") for i in range(2)]
-        for i in range(2):
-            cols = slice(i * HALF, (i + 1) * HALF)
-            nc.sync.dma_start(e1_half[i][:], e1[:, cols].broadcast_to([P, HALF]))
-            nc.sync.dma_start(e2_half[i][:], e2[:, cols].broadcast_to([P, HALF]))
+        nc.sync.dma_start(e1_half[0][:], e1[:, 0:HALF].broadcast_to([P, HALF]))
+        nc.sync.dma_start(e2_half[0][:], e2[:, 0:HALF].broadcast_to([P, HALF]))
+        w_out_sb = held.tile([P, P], BF16, name="w_out_sb")
+        nc.sync.dma_start(w_out_sb[:], w_out)
+        b_out_sb = held.tile([P, 1], F32, name="b_out_sb")
+        nc.sync.dma_start(b_out_sb[:], b_out)
+        nc.sync.dma_start(e1_half[1][:], e1[:, HALF:N].broadcast_to([P, HALF]))
+        nc.sync.dma_start(e2_half[1][:], e2[:, HALF:N].broadcast_to([P, HALF]))
 
         zeros = held.tile([P, BANK], BF16, name="zeros")
         nc.vector.memset(zeros[:], 0.0)

@@ -45,12 +45,12 @@ def tile_vectorfield_g_kernel(tc, z, w_in, b_in, pooled, cb, e1, e2, w_out, b_ou
         e2_half = [held.tile([P, HALF], F32, name=f"e2_half{i}") for i in range(2)]
         nc.sync.dma_start(e1_half[0][:], e1[:, 0:HALF].broadcast_to([P, HALF]))
         nc.sync.dma_start(e2_half[0][:], e2[:, 0:HALF].broadcast_to([P, HALF]))
+        nc.sync.dma_start(e1_half[1][:], e1[:, HALF:N].broadcast_to([P, HALF]))
+        nc.sync.dma_start(e2_half[1][:], e2[:, HALF:N].broadcast_to([P, HALF]))
         w_out_sb = held.tile([P, P], BF16, name="w_out_sb")
         nc.sync.dma_start(w_out_sb[:], w_out)
         b_out_sb = held.tile([P, 1], F32, name="b_out_sb")
         nc.sync.dma_start(b_out_sb[:], b_out)
-        nc.sync.dma_start(e1_half[1][:], e1[:, HALF:N].broadcast_to([P, HALF]))
-        nc.sync.dma_start(e2_half[1][:], e2[:, HALF:N].broadcast_to([P, HALF]))
 
         zeros = held.tile([P, BANK], BF16, name="zeros")
         nc.vector.memset(zeros[:], 0.0)
@@ -66,7 +66,7 @@ def tile_vectorfield_g_kernel(tc, z, w_in, b_in, pooled, cb, e1, e2, w_out, b_ou
             picked = z_sb[:].indirect(offsets[:, k * PIECE // 16 : (k + 1) * PIECE // 16])
             nc.tensor.matmul(h_ps[k][:], w_in_sb[:], picked, start=True, stop=True)
 
-        for k in range(PIECES):
+        def products(k):
             half, first = divmod(k * PIECE, HALF)
             e_cols = slice(first, first + PIECE)
 
@@ -85,13 +85,22 @@ def tile_vectorfield_g_kernel(tc, z, w_in, b_in, pooled, cb, e1, e2, w_out, b_ou
             nc.vector.scalar_tensor_tensor(
                 t2[:], u_ps[:, PIECE : 2 * PIECE], cb_sb[:, 1:2], e2_half[half][:, e_cols], op0=ADD, op1=MULT
             )
+            return t1, t2
+
+        def finish(k, t1, t2):
             mixed = work.tile([P, PIECE], F32, name="mixed")
             nc.vector.tensor_tensor(mixed[:], t1[:], t2[:], SUBTRACT)
             y_sb = work.tile([P, PIECE], BF16, name="y_sb")
             nc.scalar.activation(y_sb[:], mixed[:], TANH)
-
             o_ps = psum.tile([P, PIECE], F32, name="o_ps")
             nc.tensor.matmul(o_ps[:], w_out_sb[:], y_sb[:], start=True, stop=True)
             o_sb = work.tile([P, PIECE], F32, name="o_sb")
             nc.scalar.activation(o_sb[:], o_ps[:], TANH, bias=b_out_sb[:])
             nc.sync.dma_start(out[:, k * PIECE : (k + 1) * PIECE], o_sb[:])
+
+        waiting = products(0)
+        for k in range(1, PIECES):
+            following = products(k)
+            finish(k - 1, *waiting)
+            waiting = following
+        finish(PIECES - 1, *waiting)

@@ -15,8 +15,6 @@ N = 1024
 PIECE = 256
 PIECES = N // PIECE
 HALF = N // 2
-BANK = 512
-WARM_MATMULS = 3
 FLOPS = 2 * N * (P * P + P * 2 * P + P * P)
 
 
@@ -45,28 +43,24 @@ def tile_vectorfield_g_kernel(tc, z, w_in, b_in, pooled, cb, e1, e2, w_out, b_ou
         e2_half = [held.tile([P, HALF], F32, name=f"e2_half{i}") for i in range(2)]
         nc.sync.dma_start(e1_half[0][:], e1[:, 0:HALF].broadcast_to([P, HALF]))
         nc.sync.dma_start(e2_half[0][:], e2[:, 0:HALF].broadcast_to([P, HALF]))
-        nc.sync.dma_start(e1_half[1][:], e1[:, HALF:N].broadcast_to([P, HALF]))
-        nc.sync.dma_start(e2_half[1][:], e2[:, HALF:N].broadcast_to([P, HALF]))
         w_out_sb = held.tile([P, P], BF16, name="w_out_sb")
         nc.sync.dma_start(w_out_sb[:], w_out)
         b_out_sb = held.tile([P, 1], F32, name="b_out_sb")
         nc.sync.dma_start(b_out_sb[:], b_out)
+        nc.sync.dma_start(e1_half[1][:], e1[:, HALF:N].broadcast_to([P, HALF]))
+        nc.sync.dma_start(e2_half[1][:], e2[:, HALF:N].broadcast_to([P, HALF]))
 
-        zeros = held.tile([P, BANK], BF16, name="zeros")
+        zeros = held.tile([P, 1], BF16, name="zeros")
         nc.vector.memset(zeros[:], 0.0)
         warm_sb = held.tile([P, 1], F32, name="warm_sb")
         nc.scalar.activation(warm_sb[:], zeros[:, 0:1], TANH)
-
-        warm_ps = psum.tile([P, BANK], F32, name="warm_ps", tag="o_ps")
-        for i in range(WARM_MATMULS):
-            nc.tensor.matmul(warm_ps[:], zeros[:, 0:P], zeros[:], start=True, stop=True)
 
         h_ps = [psum_h.tile([P, PIECE], F32, name="h_ps") for k in range(PIECES)]
         for k in range(PIECES):
             picked = z_sb[:].indirect(offsets[:, k * PIECE // 16 : (k + 1) * PIECE // 16])
             nc.tensor.matmul(h_ps[k][:], w_in_sb[:], picked, start=True, stop=True)
 
-        def products(k):
+        for k in range(PIECES):
             half, first = divmod(k * PIECE, HALF)
             e_cols = slice(first, first + PIECE)
 
@@ -85,22 +79,13 @@ def tile_vectorfield_g_kernel(tc, z, w_in, b_in, pooled, cb, e1, e2, w_out, b_ou
             nc.vector.scalar_tensor_tensor(
                 t2[:], u_ps[:, PIECE : 2 * PIECE], cb_sb[:, 1:2], e2_half[half][:, e_cols], op0=ADD, op1=MULT
             )
-            return t1, t2
-
-        def finish(k, t1, t2):
             mixed = work.tile([P, PIECE], F32, name="mixed")
             nc.vector.tensor_tensor(mixed[:], t1[:], t2[:], SUBTRACT)
             y_sb = work.tile([P, PIECE], BF16, name="y_sb")
             nc.scalar.activation(y_sb[:], mixed[:], TANH)
+
             o_ps = psum.tile([P, PIECE], F32, name="o_ps")
             nc.tensor.matmul(o_ps[:], w_out_sb[:], y_sb[:], start=True, stop=True)
             o_sb = work.tile([P, PIECE], F32, name="o_sb")
             nc.scalar.activation(o_sb[:], o_ps[:], TANH, bias=b_out_sb[:])
             nc.sync.dma_start(out[:, k * PIECE : (k + 1) * PIECE], o_sb[:])
-
-        waiting = products(0)
-        for k in range(1, PIECES):
-            following = products(k)
-            finish(k - 1, *waiting)
-            waiting = following
-        finish(PIECES - 1, *waiting)

@@ -23,8 +23,8 @@ def tile_vectorfield_g_kernel(tc, z, w_in, b_in, pooled, cb, e1, e2, w_out, b_ou
     with (
         tc.tile_pool(name="held", bufs=1) as held,
         tc.tile_pool(name="work", bufs=PIECES) as work,
-        tc.psum_pool(name="psum_h", bufs=PIECES) as psum_h,
-        tc.psum_pool(name="psum", bufs=2) as psum,
+        tc.psum_pool(name="psum_ends", bufs=PIECES) as psum_ends,
+        tc.psum_pool(name="psum_u", bufs=2) as psum_u,
     ):
         z_sb = held.tile([P, S], BF16, name="z_sb")
         nc.sync.dma_start(z_sb[:], z)
@@ -55,7 +55,7 @@ def tile_vectorfield_g_kernel(tc, z, w_in, b_in, pooled, cb, e1, e2, w_out, b_ou
         warm_sb = held.tile([P, 1], F32, name="warm_sb")
         nc.scalar.activation(warm_sb[:], zeros[:, 0:1], TANH)
 
-        h_ps = [psum_h.tile([P, PIECE], F32, name="h_ps") for k in range(PIECES)]
+        h_ps = [psum_ends.tile([P, PIECE], F32, name="h_ps", tag="ends") for k in range(PIECES)]
         for k in range(PIECES):
             picked = z_sb[:].indirect(offsets[:, k * PIECE // 16 : (k + 1) * PIECE // 16])
             nc.tensor.matmul(h_ps[k][:], w_in_sb[:], picked, start=True, stop=True)
@@ -67,24 +67,25 @@ def tile_vectorfield_g_kernel(tc, z, w_in, b_in, pooled, cb, e1, e2, w_out, b_ou
             h_sb = work.tile([P, PIECE], BF16, name="h_sb")
             nc.scalar.activation(h_sb[:], h_ps[k][:], RELU, bias=b_in_sb[:])
 
-            u_ps = psum.tile([P, 2 * PIECE], F32, name="u_ps")
-            nc.tensor.matmul(u_ps[:, 0:PIECE], pooled_sb[:, 0:P], h_sb[:], start=True, stop=True)
-            nc.tensor.matmul(u_ps[:, PIECE : 2 * PIECE], pooled_sb[:, P : 2 * P], h_sb[:], start=True, stop=True)
+            u1_ps = psum_u.tile([P, PIECE], F32, name="u1_ps")
+            nc.tensor.matmul(u1_ps[:], pooled_sb[:, 0:P], h_sb[:], start=True, stop=True)
+            u2_ps = psum_u.tile([P, PIECE], F32, name="u2_ps")
+            nc.tensor.matmul(u2_ps[:], pooled_sb[:, P : 2 * P], h_sb[:], start=True, stop=True)
 
             t1 = work.tile([P, PIECE], F32, name="t1")
             nc.vector.scalar_tensor_tensor(
-                t1[:], u_ps[:, 0:PIECE], cb_sb[:, 0:1], e1_half[half][:, e_cols], op0=ADD, op1=MULT
+                t1[:], u1_ps[:], cb_sb[:, 0:1], e1_half[half][:, e_cols], op0=ADD, op1=MULT
             )
             t2 = work.tile([P, PIECE], F32, name="t2")
             nc.vector.scalar_tensor_tensor(
-                t2[:], u_ps[:, PIECE : 2 * PIECE], cb_sb[:, 1:2], e2_half[half][:, e_cols], op0=ADD, op1=MULT
+                t2[:], u2_ps[:], cb_sb[:, 1:2], e2_half[half][:, e_cols], op0=ADD, op1=MULT
             )
             mixed = work.tile([P, PIECE], F32, name="mixed")
             nc.vector.tensor_tensor(mixed[:], t1[:], t2[:], SUBTRACT)
             y_sb = work.tile([P, PIECE], BF16, name="y_sb")
             nc.scalar.activation(y_sb[:], mixed[:], TANH)
 
-            o_ps = psum.tile([P, PIECE], F32, name="o_ps")
+            o_ps = psum_ends.tile([P, PIECE], F32, name="o_ps", tag="ends")
             nc.tensor.matmul(o_ps[:], w_out_sb[:], y_sb[:], start=True, stop=True)
             o_sb = work.tile([P, PIECE], F32, name="o_sb")
             nc.scalar.activation(o_sb[:], o_ps[:], TANH, bias=b_out_sb[:])

@@ -14,7 +14,6 @@ S = 512
 N = 1024
 PIECE = 256
 PIECES = N // PIECE
-HALF = N // 2
 FLOPS = 2 * N * (P * P + P * 2 * P + P * P)
 
 
@@ -39,16 +38,14 @@ def tile_vectorfield_g_kernel(tc, z, w_in, b_in, pooled, cb, e1, e2, w_out, b_ou
         cb_sb = held.tile([P, 2], F32, name="cb_sb")
         with nc.allow_non_contiguous_dma(reason="two bias columns, one float32 to a partition each"):
             nc.scalar.dma_start(cb_sb[:], cb.rearrange("(t p) o -> p (t o)", t=2))
-        e1_half = [held.tile([P, HALF], F32, name=f"e1_half{i}") for i in range(2)]
-        e2_half = [held.tile([P, HALF], F32, name=f"e2_half{i}") for i in range(2)]
-        nc.sync.dma_start(e1_half[0][:], e1[:, 0:HALF].broadcast_to([P, HALF]))
-        nc.sync.dma_start(e2_half[0][:], e2[:, 0:HALF].broadcast_to([P, HALF]))
+        e1_sb = held.tile([P, N], F32, name="e1_sb")
+        nc.sync.dma_start(e1_sb[:], e1.broadcast_to([P, N]))
+        e2_sb = held.tile([P, N], F32, name="e2_sb")
+        nc.sync.dma_start(e2_sb[:], e2.broadcast_to([P, N]))
         w_out_sb = held.tile([P, P], BF16, name="w_out_sb")
         nc.sync.dma_start(w_out_sb[:], w_out)
         b_out_sb = held.tile([P, 1], F32, name="b_out_sb")
         nc.sync.dma_start(b_out_sb[:], b_out)
-        nc.sync.dma_start(e1_half[1][:], e1[:, HALF:N].broadcast_to([P, HALF]))
-        nc.sync.dma_start(e2_half[1][:], e2[:, HALF:N].broadcast_to([P, HALF]))
 
         zeros = held.tile([P, 1], BF16, name="zeros")
         nc.vector.memset(zeros[:], 0.0)
@@ -61,8 +58,7 @@ def tile_vectorfield_g_kernel(tc, z, w_in, b_in, pooled, cb, e1, e2, w_out, b_ou
             nc.tensor.matmul(h_ps[k][:], w_in_sb[:], picked, start=True, stop=True)
 
         for k in range(PIECES):
-            half, first = divmod(k * PIECE, HALF)
-            e_cols = slice(first, first + PIECE)
+            cols = slice(k * PIECE, (k + 1) * PIECE)
 
             h_sb = work.tile([P, PIECE], BF16, name="h_sb")
             nc.scalar.activation(h_sb[:], h_ps[k][:], RELU, bias=b_in_sb[:])
@@ -74,11 +70,11 @@ def tile_vectorfield_g_kernel(tc, z, w_in, b_in, pooled, cb, e1, e2, w_out, b_ou
 
             t1 = work.tile([P, PIECE], F32, name="t1")
             nc.vector.scalar_tensor_tensor(
-                t1[:], u1_ps[:], cb_sb[:, 0:1], e1_half[half][:, e_cols], op0=ADD, op1=MULT
+                t1[:], u1_ps[:], cb_sb[:, 0:1], e1_sb[:, cols], op0=ADD, op1=MULT
             )
             t2 = work.tile([P, PIECE], F32, name="t2")
             nc.vector.scalar_tensor_tensor(
-                t2[:], u2_ps[:], cb_sb[:, 1:2], e2_half[half][:, e_cols], op0=ADD, op1=MULT
+                t2[:], u2_ps[:], cb_sb[:, 1:2], e2_sb[:, cols], op0=ADD, op1=MULT
             )
             mixed = work.tile([P, PIECE], F32, name="mixed")
             nc.vector.tensor_tensor(mixed[:], t1[:], t2[:], SUBTRACT)
@@ -89,4 +85,4 @@ def tile_vectorfield_g_kernel(tc, z, w_in, b_in, pooled, cb, e1, e2, w_out, b_ou
             nc.tensor.matmul(o_ps[:], w_out_sb[:], y_sb[:], start=True, stop=True)
             o_sb = work.tile([P, PIECE], F32, name="o_sb")
             nc.scalar.activation(o_sb[:], o_ps[:], TANH, bias=b_out_sb[:])
-            nc.sync.dma_start(out[:, k * PIECE : (k + 1) * PIECE], o_sb[:])
+            nc.sync.dma_start(out[:, cols], o_sb[:])

@@ -12,8 +12,11 @@ SUBTRACT = mybir.AluOpType.subtract
 P = 128
 S = 512
 N = 1024
-PIECE = 256
-PIECES = N // PIECE
+WIDTHS = (256, 384, 256, 128)
+PIECES = len(WIDTHS)
+FIRSTS = [sum(WIDTHS[:k]) for k in range(PIECES)]
+WIDEST = max(WIDTHS)
+BANK = 512
 FLOPS = 2 * N * (P * P + P * 2 * P + P * P)
 
 
@@ -52,37 +55,38 @@ def tile_vectorfield_g_kernel(tc, z, w_in, b_in, pooled, cb, e1, e2, w_out, b_ou
         warm_sb = held.tile([P, 1], F32, name="warm_sb")
         nc.scalar.activation(warm_sb[:], zeros[:, 0:1], TANH)
 
-        h_ps = [psum_ends.tile([P, PIECE], F32, name="h_ps", tag="ends") for k in range(PIECES)]
+        h_ps = [psum_ends.tile([P, BANK], F32, name="h_ps", tag="ends") for k in range(PIECES)]
         for k in range(PIECES):
-            picked = z_sb[:].indirect(offsets[:, k * PIECE // 16 : (k + 1) * PIECE // 16])
-            nc.tensor.matmul(h_ps[k][:], w_in_sb[:], picked, start=True, stop=True)
+            picked = z_sb[:].indirect(offsets[:, FIRSTS[k] // 16 : (FIRSTS[k] + WIDTHS[k]) // 16])
+            nc.tensor.matmul(h_ps[k][:, 0 : WIDTHS[k]], w_in_sb[:], picked, start=True, stop=True)
 
         for k in range(PIECES):
-            cols = slice(k * PIECE, (k + 1) * PIECE)
+            width = WIDTHS[k]
+            cols = slice(FIRSTS[k], FIRSTS[k] + width)
 
-            h_sb = work.tile([P, PIECE], BF16, name="h_sb")
-            nc.scalar.activation(h_sb[:], h_ps[k][:], RELU, bias=b_in_sb[:])
+            h_sb = work.tile([P, WIDEST], BF16, name="h_sb")
+            nc.scalar.activation(h_sb[:, 0:width], h_ps[k][:, 0:width], RELU, bias=b_in_sb[:])
 
-            u1_ps = psum_u.tile([P, PIECE], F32, name="u1_ps")
-            nc.tensor.matmul(u1_ps[:], pooled_sb[:, 0:P], h_sb[:], start=True, stop=True)
-            u2_ps = psum_u.tile([P, PIECE], F32, name="u2_ps")
-            nc.tensor.matmul(u2_ps[:], pooled_sb[:, P : 2 * P], h_sb[:], start=True, stop=True)
+            u1_ps = psum_u.tile([P, BANK], F32, name="u1_ps")
+            nc.tensor.matmul(u1_ps[:, 0:width], pooled_sb[:, 0:P], h_sb[:, 0:width], start=True, stop=True)
+            u2_ps = psum_u.tile([P, BANK], F32, name="u2_ps")
+            nc.tensor.matmul(u2_ps[:, 0:width], pooled_sb[:, P : 2 * P], h_sb[:, 0:width], start=True, stop=True)
 
-            t1 = work.tile([P, PIECE], F32, name="t1")
+            t1 = work.tile([P, WIDEST], F32, name="t1")
             nc.vector.scalar_tensor_tensor(
-                t1[:], u1_ps[:], cb_sb[:, 0:1], e1_sb[:, cols], op0=ADD, op1=MULT
+                t1[:, 0:width], u1_ps[:, 0:width], cb_sb[:, 0:1], e1_sb[:, cols], op0=ADD, op1=MULT
             )
-            t2 = work.tile([P, PIECE], F32, name="t2")
+            t2 = work.tile([P, WIDEST], F32, name="t2")
             nc.vector.scalar_tensor_tensor(
-                t2[:], u2_ps[:], cb_sb[:, 1:2], e2_sb[:, cols], op0=ADD, op1=MULT
+                t2[:, 0:width], u2_ps[:, 0:width], cb_sb[:, 1:2], e2_sb[:, cols], op0=ADD, op1=MULT
             )
-            mixed = work.tile([P, PIECE], F32, name="mixed")
-            nc.vector.tensor_tensor(mixed[:], t1[:], t2[:], SUBTRACT)
-            y_sb = work.tile([P, PIECE], BF16, name="y_sb")
-            nc.scalar.activation(y_sb[:], mixed[:], TANH)
+            mixed = work.tile([P, WIDEST], F32, name="mixed")
+            nc.vector.tensor_tensor(mixed[:, 0:width], t1[:, 0:width], t2[:, 0:width], SUBTRACT)
+            y_sb = work.tile([P, WIDEST], BF16, name="y_sb")
+            nc.scalar.activation(y_sb[:, 0:width], mixed[:, 0:width], TANH)
 
-            o_ps = psum_ends.tile([P, PIECE], F32, name="o_ps", tag="ends")
-            nc.tensor.matmul(o_ps[:], w_out_sb[:], y_sb[:], start=True, stop=True)
-            o_sb = work.tile([P, PIECE], F32, name="o_sb")
-            nc.scalar.activation(o_sb[:], o_ps[:], TANH, bias=b_out_sb[:])
-            nc.sync.dma_start(out[:, cols], o_sb[:])
+            o_ps = psum_ends.tile([P, BANK], F32, name="o_ps", tag="ends")
+            nc.tensor.matmul(o_ps[:, 0:width], w_out_sb[:], y_sb[:, 0:width], start=True, stop=True)
+            o_sb = work.tile([P, WIDEST], F32, name="o_sb")
+            nc.scalar.activation(o_sb[:, 0:width], o_ps[:, 0:width], TANH, bias=b_out_sb[:])
+            nc.sync.dma_start(out[:, cols], o_sb[:, 0:width])

@@ -29,11 +29,11 @@ def tile_vectorfield_g_kernel(tc, z, w_in, b_in, pooled, cb, e1, e2, w_out, b_ou
         tc.psum_pool(name="psum_u", bufs=2) as psum_u,
     ):
         z_sb = held.tile([P, S], BF16, name="z_sb")
-        nc.sync.dma_start(z_sb[:], z)
+        nc.scalar.dma_start(z_sb[:], z)
         offsets = held.tile([P, N // 16], U16, name="offsets")
         nc.sync.dma_start(offsets[:], offs)
         w_in_sb = held.tile([P, P], BF16, name="w_in_sb")
-        nc.scalar.dma_start(w_in_sb[:], w_in)
+        nc.sync.dma_start(w_in_sb[:], w_in)
         b_in_sb = held.tile([P, 1], F32, name="b_in_sb")
         nc.scalar.dma_start(b_in_sb[:], b_in)
         pooled_sb = held.tile([P, 2 * P], BF16, name="pooled_sb")

import concourse.mybir as mybir

BF16 = mybir.dt.bfloat16
F32 = mybir.dt.float32
U16 = mybir.dt.uint16
RELU = mybir.ActivationFunctionType.Relu
TANH = mybir.ActivationFunctionType.Tanh
ADD = mybir.AluOpType.add
MULT = mybir.AluOpType.mult
SUBTRACT = mybir.AluOpType.subtract

P = 128
S = 512
N = 1024
WIDTHS = (256, 384, 256, 128)
PIECES = len(WIDTHS)
FIRSTS = [sum(WIDTHS[:k]) for k in range(PIECES)]
WIDEST = max(WIDTHS)
BANK = 512
FLOPS = 2 * N * (P * P + P * 2 * P + P * P)


def tile_vectorfield_g_kernel(tc, z, w_in, b_in, pooled, cb, e1, e2, w_out, b_out, offs, out):
    nc = tc.nc
    with (
        tc.tile_pool(name="held", bufs=1) as held,
        tc.tile_pool(name="work", bufs=PIECES) as work,
        tc.psum_pool(name="psum_ends", bufs=PIECES) as psum_ends,
        tc.psum_pool(name="psum_u", bufs=2) as psum_u,
    ):
        z_sb = held.tile([P, S], BF16, name="z_sb")
        nc.scalar.dma_start(z_sb[:], z)
        offsets = held.tile([P, N // 16], U16, name="offsets")
        nc.sync.dma_start(offsets[:], offs)
        w_in_sb = held.tile([P, P], BF16, name="w_in_sb")
        nc.sync.dma_start(w_in_sb[:], w_in)
        b_in_sb = held.tile([P, 1], F32, name="b_in_sb")
        nc.scalar.dma_start(b_in_sb[:], b_in)
        pooled_sb = held.tile([P, 2 * P], BF16, name="pooled_sb")
        nc.scalar.dma_start(pooled_sb[:], pooled)
        cb_sb = held.tile([P, 2], F32, name="cb_sb")
        with nc.allow_non_contiguous_dma(reason="two bias columns, one float32 to a partition each"):
            nc.scalar.dma_start(cb_sb[:], cb.rearrange("(t p) o -> p (t o)", t=2))
        e1_sb = held.tile([P, N], F32, name="e1_sb")
        nc.sync.dma_start(e1_sb[:], e1.broadcast_to([P, N]))
        e2_sb = held.tile([P, N], F32, name="e2_sb")
        nc.sync.dma_start(e2_sb[:], e2.broadcast_to([P, N]))
        w_out_sb = held.tile([P, P], BF16, name="w_out_sb")
        nc.sync.dma_start(w_out_sb[:], w_out)
        b_out_sb = held.tile([P, 1], F32, name="b_out_sb")
        nc.sync.dma_start(b_out_sb[:], b_out)

        zeros = held.tile([P, 1], BF16, name="zeros")
        nc.vector.memset(zeros[:], 0.0)
        warm_sb = held.tile([P, 1], F32, name="warm_sb")
        nc.scalar.activation(warm_sb[:], zeros[:, 0:1], TANH)

        h_ps = [psum_ends.tile([P, BANK], F32, name="h_ps", tag="ends") for k in range(PIECES)]
        for k in range(PIECES):
            picked = z_sb[:].indirect(offsets[:, FIRSTS[k] // 16 : (FIRSTS[k] + WIDTHS[k]) // 16])
            nc.tensor.matmul(h_ps[k][:, 0 : WIDTHS[k]], w_in_sb[:], picked, start=True, stop=True)

        for k in range(PIECES):
            width = WIDTHS[k]
            cols = slice(FIRSTS[k], FIRSTS[k] + width)

            h_sb = work.tile([P, WIDEST], BF16, name="h_sb")
            nc.scalar.activation(h_sb[:, 0:width], h_ps[k][:, 0:width], RELU, bias=b_in_sb[:])

            u1_ps = psum_u.tile([P, BANK], F32, name="u1_ps")
            nc.tensor.matmul(u1_ps[:, 0:width], pooled_sb[:, 0:P], h_sb[:, 0:width], start=True, stop=True)
            u2_ps = psum_u.tile([P, BANK], F32, name="u2_ps")
            nc.tensor.matmul(u2_ps[:, 0:width], pooled_sb[:, P : 2 * P], h_sb[:, 0:width], start=True, stop=True)

            t1 = work.tile([P, WIDEST], F32, name="t1")
            nc.vector.scalar_tensor_tensor(
                t1[:, 0:width], u1_ps[:, 0:width], cb_sb[:, 0:1], e1_sb[:, cols], op0=ADD, op1=MULT
            )
            t2 = work.tile([P, WIDEST], F32, name="t2")
            nc.vector.scalar_tensor_tensor(
                t2[:, 0:width], u2_ps[:, 0:width], cb_sb[:, 1:2], e2_sb[:, cols], op0=ADD, op1=MULT
            )
            mixed = work.tile([P, WIDEST], F32, name="mixed")
            nc.vector.tensor_tensor(mixed[:, 0:width], t1[:, 0:width], t2[:, 0:width], SUBTRACT)
            y_sb = work.tile([P, WIDEST], BF16, name="y_sb")
            nc.scalar.activation(y_sb[:, 0:width], mixed[:, 0:width], TANH)

            o_ps = psum_ends.tile([P, BANK], F32, name="o_ps", tag="ends")
            nc.tensor.matmul(o_ps[:, 0:width], w_out_sb[:], y_sb[:, 0:width], start=True, stop=True)
            o_sb = work.tile([P, WIDEST], F32, name="o_sb")
            nc.scalar.activation(o_sb[:, 0:width], o_ps[:, 0:width], TANH, bias=b_out_sb[:])
            nc.sync.dma_start(out[:, cols], o_sb[:, 0:width])
